import numpy as np
import ml_dtypes


def mxq(x, axis, fmt="e4m3"):
    dtype, down = {"e4m3": (ml_dtypes.float8_e4m3fn, 7), "e5m2": (ml_dtypes.float8_e5m2, 14)}[fmt]
    v = np.moveaxis(np.asarray(x, np.float32).astype(ml_dtypes.bfloat16).astype(np.float64), axis, -1)
    blocks = v.reshape(v.shape[:-1] + (-1, 32))
    amax = np.abs(blocks).max(-1, keepdims=True)
    byte = np.maximum(np.where(amax > 0, np.frexp(amax)[1] - 1 + 127, 0) - down, 1)
    scale = np.exp2(byte - 127.0)
    codes = (blocks / scale).astype(np.float32).astype(dtype).astype(np.float64)
    return np.moveaxis((codes * scale).reshape(v.shape), -1, axis)


WIDE = False


def mx_kscale(k):
    if not WIDE:
        return np.ones(k)
    levels = np.array([10, -10, 5, -5, 0])
    if k % 512:
        return np.exp2(np.random.permutation(np.resize(levels, k // 32))).repeat(32)
    a = np.empty((k // 512, 16))
    for p in range(k // 512):
        a[p, :8] = np.random.permutation(np.resize(levels, 8))
        for g in range(8):
            far = levels[np.abs(levels - a[p, g]) >= 10]
            a[p, g + 8] = far[np.random.randint(len(far))]
    return np.exp2(a.ravel()).repeat(32)


BF16 = ml_dtypes.bfloat16


def bf(x):
    return np.asarray(x, np.float32).astype(BF16)


def f64(x):
    return np.asarray(x).astype(np.float64)


B, T, HP, WP, NH, D, DFF = 16, 8, 3, 4, 16, 1024, 4096
HW = HP * WP


def setup_inputs():
    s = mx_kscale(D)
    c = np.random.standard_normal((B * T, 1 + HW, D)) * 1.5 / np.sqrt(1 + HW)
    c[:, 0, :] *= 5.0
    return {"ctx_s": bf(c * s),
            "x_res": bf(np.random.standard_normal((B, 1 + HW * T, D)) * 1.1),
            "s_out_w": bf(np.random.standard_normal((D, D)) / np.sqrt(D) / s[:, None]),
            "s_out_b": bf(0.1 * np.random.standard_normal(D))}


def reference(ctx_s, x_res, s_out_w, s_out_b):
    res_s = (mxq(f64(ctx_s), 2, "e4m3") @ mxq(f64(s_out_w), 0, "e4m3")) + f64(s_out_b)
    cls_tok = res_s[:, 0, :].reshape(B, T, D).mean(axis=1, keepdims=True)
    res_p = res_s[:, 1:, :].reshape(B, T, HW, D).swapaxes(1, 2).reshape(B, HW * T, D)
    return f64(x_res) + np.concatenate([cls_tok, res_p], axis=1)

@@ -1,0 +1,268 @@
+from contextlib import ExitStack
+
+import concourse.mybir as mybir
+from concourse.masks import make_identity
+
+F32 = mybir.dt.float32
+BF16 = mybir.dt.bfloat16
+I32 = mybir.dt.int32
+U32 = mybir.dt.uint32
+U8 = mybir.dt.uint8
+FP8X4 = mybir.dt.float8_e4m3fn_x4
+ADD = mybir.AluOpType.add
+MULT = mybir.AluOpType.mult
+
+P = 128
+SAMPLES = 16
+FRAMES = 8
+PATCHES = 12
+TOKENS = 1 + PATCHES
+D = 1024
+K_PASS = 512
+PASSES = D // K_PASS
+BANK = 512
+HALVES = D // BANK
+WORDS = D // 2
+BLOCKS = WORDS // P
+CHUNK = 2
+RUN = 4
+W_VECTOR_COLS = 256
+VECTOR_EVERY = 2
+
+FLOPS = 2 * P * TOKENS * D * D
+
+
+def tile_timesformerlayer_pc_kernel(tc, ctx_s, x_res, s_out_w, s_out_b, out):
+    nc = tc.nc
+    token_groups = [[0], [1]] + [[j, j + 1] for j in range(2, TOKENS - 1, 2)] + [[TOKENS - 1]]
+    halves = [slice(h * BANK, (h + 1) * BANK) for h in range(HALVES)]
+
+    with ExitStack() as stack:
+        keep = stack.enter_context(tc.tile_pool(name="keep", bufs=1))
+        work = stack.enter_context(tc.tile_pool(name="work", bufs=3))
+        psum_bias = stack.enter_context(tc.psum_pool(name="psum_bias", bufs=1))
+        psum_turn = stack.enter_context(tc.psum_pool(name="psum_turn", bufs=2))
+        psum_acc = stack.enter_context(tc.psum_pool(name="psum_acc", bufs=4))
+        stack.enter_context(tc.manual_schedule())
+
+        ident = keep.tile([P, P], F32)
+        ones = keep.tile([P, P], BF16)
+        bias_row = keep.tile([1, D], BF16)
+        bias_rows = keep.tile([P, D], BF16)
+        bias_sbuf = keep.tile([P, D], F32)
+        bias_psum = [psum_bias.tile([P, BANK], F32, name="bias_psum%d" % h) for h in range(HALVES)]
+        ctx_chunks = [
+            keep.tile([P, min(CHUNK, TOKENS - first) * D], BF16, name="ctx%d" % first)
+            for first in range(0, TOKENS, CHUNK)
+        ]
+        w_raw = [keep.tile([P, 4, D], BF16, name="w_raw%d" % g) for g in range(PASSES)]
+        w_grouped = [
+            keep.tile([P, D, 4], BF16, name="w_grouped%d" % g, align_bytes=64) for g in range(PASSES)
+        ]
+        w_codes = [keep.tile([P, D], U32, name="w_codes%d" % g, align_bytes=64) for g in range(PASSES)]
+        w_scales = [keep.tile([P, D], U8, name="w_scales%d" % g, align_bytes=64) for g in range(PASSES)]
+        x_patch = [keep.tile([P, D], BF16, name="x_patch%d" % p) for p in range(PATCHES)]
+        y_patch = [keep.tile([P, D], F32, name="y_patch%d" % p) for p in range(PATCHES)]
+        x_class = keep.tile([P, P], BF16)
+        bias_class = keep.tile([P, P], BF16)
+        y_class = keep.tile([P, P], F32)
+        class_sums = keep.tile([P, P], F32)
+
+        def patch_rows(dram, p):
+            return dram[:, 1 + p * FRAMES : 1 + (p + 1) * FRAMES, :]
+
+        def class_rows(dram):
+            return dram[:, 0, :].rearrange("b (c n) -> c b n", n=P)
+
+        nc.vector.memset(bias_rows[:].bitcast(I32), 0)
+        nc.vector.memset(ones[:], 1.0)
+        make_identity(nc, ident[:])
+
+        def load_ctx(c):
+            first = c * CHUNK
+            last = min(first + CHUNK, TOKENS)
+            nc.sync.dma_start(
+                out=ctx_chunks[c][:], in_=ctx_s[:, first:last, :].rearrange("s j d -> s (j d)")
+            )
+
+        def load_w(g):
+            rows = s_out_w[g * K_PASS : (g + 1) * K_PASS, :]
+            nc.sync.dma_start(out=w_raw[g][:], in_=rows.rearrange("(p t) n -> p t n", t=4))
+
+        def load_x(p):
+            nc.sync.dma_start(out=x_patch[p][:], in_=patch_rows(x_res, p))
+
+        nc.sync.dma_start(out=bias_row[:], in_=s_out_b.rearrange("(o n) -> o n", o=1))
+        load_w(0)
+        load_x(0)
+        load_w(1)
+        load_ctx(0)
+        load_x(1)
+        nc.sync.dma_start(out=x_class[:], in_=class_rows(x_res))
+        nc.sync.dma_start(
+            out=bias_class[:],
+            in_=s_out_b.rearrange("(c o n) -> c o n", o=1, n=P).to_broadcast([D // P, SAMPLES, P]),
+        )
+        for c in range(1, len(ctx_chunks)):
+            load_ctx(c)
+            for p in range(c * CHUNK, min((c + 1) * CHUNK, PATCHES)):
+                load_x(p)
+
+        nc.vector.tensor_copy(out=bias_rows[0:1, :], in_=bias_row[:])
+        for h in range(HALVES):
+            spread = psum_acc.tile([P, BANK], F32, tag="acc")
+            for target in (spread, bias_psum[h]):
+                nc.tensor.matmul(out=target[:], lhsT=ones[:], rhs=bias_rows[:, halves[h]], start=True, stop=True)
+            nc.scalar.copy(out=bias_sbuf[:, halves[h]], in_=spread[:])
+
+        def add_bias(tokens):
+            for j in tokens:
+                p = j - 1
+                if j == 0:
+                    nc.vector.tensor_tensor(out=y_class[:], in0=x_class[:], in1=bias_class[:], op=ADD)
+                elif p % VECTOR_EVERY == VECTOR_EVERY - 1:
+                    for h in range(HALVES):
+                        nc.vector.tensor_tensor(
+                            out=y_patch[p][:, halves[h]], in0=bias_psum[h][:], in1=x_patch[p][:, halves[h]], op=ADD
+                        )
+                else:
+                    for h in range(HALVES):
+                        nc.gpsimd.tensor_tensor(
+                            out=y_patch[p][:, halves[h]],
+                            in0=x_patch[p][:, halves[h]],
+                            in1=bias_sbuf[:, halves[h]],
+                            op=ADD,
+                        )
+
+        def turn(tokens):
+            grouped = work.tile([P, len(tokens) * D], BF16, align_bytes=64, tag="grouped")
+            grouped_words = grouped[:].bitcast(F32)
+            for i, j in enumerate(tokens):
+                words = ctx_chunks[j // CHUNK][:].bitcast(F32)
+                turned = psum_turn.tile([P, BLOCKS, P], F32, tag="turned")
+                for blk in range(BLOCKS):
+                    first = (j % CHUNK) * WORDS + (blk // 2) * 2 * P
+                    nc.tensor.transpose(
+                        out=turned[:, blk, :], in_=words[:, first + blk % 2 : first + 2 * P : 2], identity=ident[:]
+                    )
+                nc.scalar.copy(
+                    out=grouped_words[:, i * WORDS : (i + 1) * WORDS].rearrange(
+                        "p (g r u) -> p g r u", g=PASSES, u=2
+                    ),
+                    in_=turned[:].rearrange("p (g u) r -> p g r u", u=2),
+                )
+            return grouped
+
+        def quantise(tokens, grouped):
+            codes = work.tile([P, len(tokens) * PASSES * P], U32, align_bytes=64, tag="codes")
+            scales = work.tile([P, len(tokens) * PASSES * P], U8, align_bytes=64, tag="scales")
+            nc.vector.quantize_mx(out=codes[:].bitcast(FP8X4), scales=scales[:], in_=grouped[:])
+            return codes, scales
+
+        def regroup_w(copy, g, first, last):
+            copy(
+                out=w_grouped[g][:, first:last, :].rearrange("p (c i) t -> p c t i", i=RUN),
+                in_=w_raw[g][:, :, first:last].rearrange("p t (c i) -> p c t i", i=RUN),
+            )
+
+        def prepare_w(g):
+            for h in range(HALVES):
+                regroup_w(nc.vector.tensor_copy, g, h * BANK, h * BANK + W_VECTOR_COLS)
+                regroup_w(nc.scalar.copy, g, h * BANK + W_VECTOR_COLS, (h + 1) * BANK)
+            for h in range(HALVES):
+                nc.vector.quantize_mx(
+                    out=w_codes[g][:, halves[h]].bitcast(FP8X4),
+                    scales=w_scales[g][:, halves[h]],
+                    in_=w_grouped[g][:, halves[h], :].rearrange("p n t -> p (n t)"),
+                )
+
+        def multiply_patch(codes, scales, i):
+            banks = []
+            for h in range(HALVES):
+                acc = psum_acc.tile([P, BANK], F32, tag="acc")
+                for g in range(PASSES):
+                    rows = slice((i * PASSES + g) * P, (i * PASSES + g + 1) * P)
+                    nc.tensor.matmul_mx(
+                        out=acc[:],
+                        lhsT=codes[:, rows].bitcast(FP8X4),
+                        lhsT_scale=scales[:, rows],
+                        rhs=w_codes[g][:, halves[h]].bitcast(FP8X4),
+                        rhs_scale=w_scales[g][:, halves[h]],
+                        start=(g == 0),
+                        stop=(g == PASSES - 1),
+                    )
+                banks.append(acc)
+            return banks
+
+        def finish_patch(p, banks):
+            for h in range(HALVES):
+                nc.vector.tensor_tensor(
+                    out=y_patch[p][:, halves[h]], in0=banks[h][:], in1=y_patch[p][:, halves[h]], op=ADD
+                )
+                nc.sync.dma_start(out=patch_rows(out, p)[:, :, halves[h]], in_=y_patch[p][:, halves[h]])
+
+        def multiply_class(codes, scales, i):
+            banks = []
+            for h in range(HALVES):
+                acc = psum_acc.tile([P, BANK], F32, tag="acc")
+                for q in range(BANK // P):
+                    cols = slice(h * BANK + q * P, h * BANK + (q + 1) * P)
+                    for g in range(PASSES):
+                        rows = slice((i * PASSES + g) * P, (i * PASSES + g + 1) * P)
+                        nc.tensor.matmul_mx(
+                            out=acc[:, q * P : (q + 1) * P],
+                            lhsT=w_codes[g][:, cols].bitcast(FP8X4),
+                            lhsT_scale=w_scales[g][:, cols],
+                            rhs=codes[:, rows].bitcast(FP8X4),
+                            rhs_scale=scales[:, rows],
+                            start=(g == 0),
+                            stop=(g == PASSES - 1),
+                        )
+                banks.append(acc)
+            return banks
+
+        def finish_class(banks):
+            per_bank = BANK // FRAMES
+            for h in range(HALVES):
+                nc.vector.tensor_reduce(
+                    out=class_sums[:, h * per_bank : (h + 1) * per_bank],
+                    in_=banks[h][:].rearrange("p (cb t) -> p cb t", t=FRAMES),
+                    axis=mybir.AxisListType.X,
+                    op=ADD,
+                )
+            back = psum_turn.tile([P, BLOCKS, P], F32, tag="turned")
+            nc.tensor.transpose(out=back[:, 0, :], in_=class_sums[:], identity=ident[:])
+            nc.vector.scalar_tensor_tensor(
+                out=y_class[:], in0=back[:, 0, :], scalar=1.0 / FRAMES, in1=y_class[:], op0=MULT, op1=ADD
+            )
+            nc.sync.dma_start(out=class_rows(out), in_=y_class[:])
+
+        def multiply(tokens, codes, scales):
+            return [
+                multiply_class(codes, scales, i) if j == 0 else multiply_patch(codes, scales, i)
+                for i, j in enumerate(tokens)
+            ]
+
+        def finish(tokens, banks):
+            for i, j in enumerate(tokens):
+                if j == 0:
+                    finish_class(banks[i])
+                else:
+                    finish_patch(j - 1, banks[i])
+
+        n_groups = len(token_groups)
+        for g in range(PASSES):
+            prepare_w(g)
+        quantised = {}
+        for u in range(2):
+            quantised[u] = quantise(token_groups[u], turn(token_groups[u]))
+            add_bias(token_groups[u])
+        for u in range(n_groups):
+            codes, scales = quantised[u]
+            banks = multiply(token_groups[u], codes, scales)
+            if u + 2 < n_groups:
+                grouped = turn(token_groups[u + 2])
+                add_bias(token_groups[u + 2])
+            finish(token_groups[u], banks)
+            if u + 2 < n_groups:
+                quantised[u + 2] = quantise(token_groups[u + 2], grouped)

@@ -10,6 +10,7 @@ U32 = mybir.dt.uint32
 U8 = mybir.dt.uint8
 FP8X4 = mybir.dt.float8_e4m3fn_x4
 ADD = mybir.AluOpType.add
+MAX = mybir.AluOpType.max
 MULT = mybir.AluOpType.mult
 
 P = 128
@@ -22,142 +23,178 @@ K_PASS = 512
 PASSES = D // K_PASS
 BANK = 512
 HALVES = D // BANK
+CHUNKS = D // P
 WORDS = D // 2
 BLOCKS = WORDS // P
-CHUNK = 2
 RUN = 4
-W_VECTOR_COLS = 256
-VECTOR_EVERY = 2
+W_VECTOR_COLS = 384
+
+ROWS = 1 + PATCHES * FRAMES
+QUADS = 4
+QUAD_ROWS = 4 * ROWS
+WINDOWS = 3
+SLOTS = 512
+LOOSE = 4
 
 FLOPS = 2 * P * TOKENS * D * D
 
 
 def tile_timesformerlayer_pc_kernel(tc, ctx_s, x_res, s_out_w, s_out_b, out):
     nc = tc.nc
-    token_groups = [[0], [1]] + [[j, j + 1] for j in range(2, TOKENS - 1, 2)] + [[TOKENS - 1]]
     halves = [slice(h * BANK, (h + 1) * BANK) for h in range(HALVES)]
+    chunks = [(0, 2), (11, 2), (2, 3), (5, 3), (8, 2), (10, 1)]
+    class_at = [ROWS * (i + 1) - 1 - P * i for i in range(WINDOWS)]
+    tiles = [(i, q) for i in range(WINDOWS) for q in range(QUADS)]
+    on_vector = 4
+    lead = 3
 
     with ExitStack() as stack:
         keep = stack.enter_context(tc.tile_pool(name="keep", bufs=1))
-        work = stack.enter_context(tc.tile_pool(name="work", bufs=3))
-        psum_bias = stack.enter_context(tc.psum_pool(name="psum_bias", bufs=1))
+        psum_x = stack.enter_context(tc.psum_pool(name="psum_x", bufs=2))
         psum_turn = stack.enter_context(tc.psum_pool(name="psum_turn", bufs=2))
         psum_acc = stack.enter_context(tc.psum_pool(name="psum_acc", bufs=4))
         stack.enter_context(tc.manual_schedule())
 
         ident = keep.tile([P, P], F32)
+        ident_b = keep.tile([P, P], BF16)
+        spread = [keep.tile([P, P], BF16, name="spread%d" % i) for i in range(WINDOWS)]
         ones = keep.tile([P, P], BF16)
         bias_row = keep.tile([1, D], BF16)
         bias_rows = keep.tile([P, D], BF16)
-        bias_sbuf = keep.tile([P, D], F32)
-        bias_psum = [psum_bias.tile([P, BANK], F32, name="bias_psum%d" % h) for h in range(HALVES)]
-        ctx_chunks = [
-            keep.tile([P, min(CHUNK, TOKENS - first) * D], BF16, name="ctx%d" % first)
-            for first in range(0, TOKENS, CHUNK)
-        ]
+        bias_idx = keep.tile([P, P], BF16)
+        ctx_chunks = [keep.tile([P, n * D], BF16, name="ctx%d" % first) for first, n in chunks]
         w_raw = [keep.tile([P, 4, D], BF16, name="w_raw%d" % g) for g in range(PASSES)]
-        w_grouped = [
-            keep.tile([P, D, 4], BF16, name="w_grouped%d" % g, align_bytes=64) for g in range(PASSES)
-        ]
+        w_grouped = [keep.tile([P, D, 4], BF16, name="w_grouped%d" % g, align_bytes=64) for g in range(PASSES)]
         w_codes = [keep.tile([P, D], U32, name="w_codes%d" % g, align_bytes=64) for g in range(PASSES)]
         w_scales = [keep.tile([P, D], U8, name="w_scales%d" % g, align_bytes=64) for g in range(PASSES)]
-        x_patch = [keep.tile([P, D], BF16, name="x_patch%d" % p) for p in range(PATCHES)]
-        y_patch = [keep.tile([P, D], F32, name="y_patch%d" % p) for p in range(PATCHES)]
-        x_class = keep.tile([P, P], BF16)
-        bias_class = keep.tile([P, P], BF16)
-        y_class = keep.tile([P, P], F32)
-        class_sums = keep.tile([P, P], F32)
+        grouped = [
+            keep.tile([P, QUADS * SLOTS * 4], BF16, name="grouped%d" % g, align_bytes=64) for g in range(PASSES)
+        ]
+        codes = [keep.tile([P, QUADS * SLOTS], U32, name="codes%d" % g, align_bytes=64) for g in range(PASSES)]
+        scales = [keep.tile([P, QUADS * SLOTS], U8, name="scales%d" % g, align_bytes=64) for g in range(PASSES)]
+        side_grouped = [keep.tile([P, PASSES * P * 4], BF16, name="side_grouped%d" % s, align_bytes=64) for s in range(2)]
+        side_codes = [keep.tile([P, PASSES * P], U32, name="side_codes%d" % s, align_bytes=64) for s in range(2)]
+        side_scales = [keep.tile([P, PASSES * P], U8, name="side_scales%d" % s, align_bytes=64) for s in range(2)]
+        side_x = [keep.tile([P, P], BF16, name="side_x%d" % s) for s in range(2)]
+        side_y = [keep.tile([P, P], F32, name="side_y%d" % s) for s in range(2)]
+        side_sums = [keep.tile([P, P], F32, name="side_sums%d" % s) for s in range(2)]
+        x_win = [keep.tile([P, QUADS, D], BF16, name="x_win%d" % i) for i in range(WINDOWS)]
+        y = [keep.tile([P, D], F32, name="y%d" % k) for k in range(len(tiles))]
 
-        def patch_rows(dram, p):
-            return dram[:, 1 + p * FRAMES : 1 + (p + 1) * FRAMES, :]
+        def rows_of(dram):
+            return dram.rearrange("b j d -> (b j) d")
 
         def class_rows(dram):
-            return dram[:, 0, :].rearrange("b (c n) -> c b n", n=P)
+            return dram[:, 0, :].rearrange("b (c n) -> b c n", n=P)
+
+        def loose_rows(dram):
+            quads = rows_of(dram).rearrange("(q r) d -> q r d", q=QUADS)
+            return quads[:, QUAD_ROWS - LOOSE :, :].rearrange("q r (c n) -> q (r c) n", n=P)
 
         nc.vector.memset(bias_rows[:].bitcast(I32), 0)
         nc.vector.memset(ones[:], 1.0)
         make_identity(nc, ident[:])
-
-        def load_ctx(c):
-            first = c * CHUNK
-            last = min(first + CHUNK, TOKENS)
-            nc.sync.dma_start(
-                out=ctx_chunks[c][:], in_=ctx_s[:, first:last, :].rearrange("s j d -> s (j d)")
+        nc.gpsimd.memset(side_grouped[1][:].bitcast(I32), 0)
+        for g in range(PASSES):
+            slots = grouped[g][:].rearrange("p (q l t) -> p q l t", q=QUADS, t=4)
+            slots = slots[:, :, ROWS - 1 : WINDOWS * ROWS + ROWS - 1, :]
+            nc.gpsimd.memset(slots.rearrange("p q (s l) t -> p q s l t", s=WINDOWS)[:, :, :, 0:1, :], 0.0)
+        nc.gpsimd.tensor_copy(out=ident_b[:], in_=ident[:])
+        for i in range(WINDOWS):
+            r = class_at[i]
+            nc.gpsimd.tensor_scalar(
+                out=spread[i][:], in0=ident_b[:], scalar1=ident[:, r : r + 1], scalar2=None, op0=MAX
             )
+
+        nc.sync.dma_start(out=bias_row[:], in_=s_out_b.rearrange("(o n) -> o n", o=1))
+        nc.scalar.dma_start(out=side_x[0][:], in_=class_rows(x_res))
+        nc.scalar.dma_start(
+            out=bias_idx[:],
+            in_=s_out_b.rearrange("(o c n) -> o c n", o=1, n=P).to_broadcast([SAMPLES, CHUNKS, P]),
+        )
+        nc.scalar.dma_start(out=side_x[1][:], in_=loose_rows(x_res))
 
         def load_w(g):
             rows = s_out_w[g * K_PASS : (g + 1) * K_PASS, :]
             nc.sync.dma_start(out=w_raw[g][:], in_=rows.rearrange("(p t) n -> p t n", t=4))
 
-        def load_x(p):
-            nc.sync.dma_start(out=x_patch[p][:], in_=patch_rows(x_res, p))
+        def load_ctx(c):
+            first, n = chunks[c]
+            nc.sync.dma_start(out=ctx_chunks[c][:], in_=ctx_s[:, first : first + n, :].rearrange("s j d -> s (j d)"))
 
-        nc.sync.dma_start(out=bias_row[:], in_=s_out_b.rearrange("(o n) -> o n", o=1))
+        def window(dram, i):
+            first = 1 + P * i
+            return rows_of(dram).rearrange("(q r) d -> r q d", q=QUADS)[first : first + P, :, :]
+
+        def load_x(i):
+            nc.sync.dma_start(out=x_win[i][:], in_=window(x_res, i))
+
         load_w(0)
-        load_x(0)
         load_w(1)
-        load_ctx(0)
-        load_x(1)
-        nc.sync.dma_start(out=x_class[:], in_=class_rows(x_res))
-        nc.sync.dma_start(
-            out=bias_class[:],
-            in_=s_out_b.rearrange("(c o n) -> c o n", o=1, n=P).to_broadcast([D // P, SAMPLES, P]),
-        )
-        for c in range(1, len(ctx_chunks)):
+        for c in range(3):
             load_ctx(c)
-            for p in range(c * CHUNK, min((c + 1) * CHUNK, PATCHES)):
-                load_x(p)
+        load_x(0)
+        for c in range(3, len(chunks)):
+            load_ctx(c)
+        load_x(1)
+        load_x(2)
 
-        nc.vector.tensor_copy(out=bias_rows[0:1, :], in_=bias_row[:])
-        for h in range(HALVES):
-            spread = psum_acc.tile([P, BANK], F32, tag="acc")
-            for target in (spread, bias_psum[h]):
-                nc.tensor.matmul(out=target[:], lhsT=ones[:], rhs=bias_rows[:, halves[h]], start=True, stop=True)
-            nc.scalar.copy(out=bias_sbuf[:, halves[h]], in_=spread[:])
+        def load_bias_row(i):
+            r = class_at[i]
+            nc.sync.dma_start(
+                out=x_win[i][r : r + 1, :, :],
+                in_=s_out_b.rearrange("(o q n) -> o q n", o=1, q=1).to_broadcast([1, QUADS, D]),
+            )
 
-        def add_bias(tokens):
-            for j in tokens:
-                p = j - 1
-                if j == 0:
-                    nc.vector.tensor_tensor(out=y_class[:], in0=x_class[:], in1=bias_class[:], op=ADD)
-                elif p % VECTOR_EVERY == VECTOR_EVERY - 1:
-                    for h in range(HALVES):
-                        nc.vector.tensor_tensor(
-                            out=y_patch[p][:, halves[h]], in0=bias_psum[h][:], in1=x_patch[p][:, halves[h]], op=ADD
-                        )
-                else:
-                    for h in range(HALVES):
-                        nc.gpsimd.tensor_tensor(
-                            out=y_patch[p][:, halves[h]],
-                            in0=x_patch[p][:, halves[h]],
-                            in1=bias_sbuf[:, halves[h]],
-                            op=ADD,
-                        )
-
-        def turn(tokens):
-            grouped = work.tile([P, len(tokens) * D], BF16, align_bytes=64, tag="grouped")
-            grouped_words = grouped[:].bitcast(F32)
-            for i, j in enumerate(tokens):
-                words = ctx_chunks[j // CHUNK][:].bitcast(F32)
-                turned = psum_turn.tile([P, BLOCKS, P], F32, tag="turned")
-                for blk in range(BLOCKS):
-                    first = (j % CHUNK) * WORDS + (blk // 2) * 2 * P
-                    nc.tensor.transpose(
-                        out=turned[:, blk, :], in_=words[:, first + blk % 2 : first + 2 * P : 2], identity=ident[:]
-                    )
-                nc.scalar.copy(
-                    out=grouped_words[:, i * WORDS : (i + 1) * WORDS].rearrange(
-                        "p (g r u) -> p g r u", g=PASSES, u=2
-                    ),
-                    in_=turned[:].rearrange("p (g u) r -> p g r u", u=2),
+        def turn(j):
+            for c, (first, n) in enumerate(chunks):
+                if first <= j < first + n:
+                    words = ctx_chunks[c][:].bitcast(F32)
+                    base = (j - first) * WORDS
+            turned = psum_turn.tile([P, BLOCKS, P], F32, tag="turned")
+            for blk in range(BLOCKS):
+                at = base + (blk // 2) * 2 * P + blk % 2
+                nc.tensor.transpose(
+                    out=turned[:, blk, :], in_=words[:, at : at + 2 * P - 1 : 2], identity=ident[:]
                 )
-            return grouped
+            return turned
 
-        def quantise(tokens, grouped):
-            codes = work.tile([P, len(tokens) * PASSES * P], U32, align_bytes=64, tag="codes")
-            scales = work.tile([P, len(tokens) * PASSES * P], U8, align_bytes=64, tag="scales")
-            nc.vector.quantize_mx(out=codes[:].bitcast(FP8X4), scales=scales[:], in_=grouped[:])
-            return codes, scales
+        def place(j, turned, copy):
+            first = (j - 1) * FRAMES
+            for g in range(PASSES):
+                slots = grouped[g][:].bitcast(F32).rearrange("p (q l u) -> p q l u", q=QUADS, u=2)
+                slots = slots[:, :, first : first + QUAD_ROWS, :].rearrange("p q (s l) u -> p q s l u", s=4)
+                copy(
+                    out=slots[:, :, :, 0:FRAMES, :],
+                    in_=turned[:, 2 * g : 2 * g + 2, :].rearrange("p u (q s t) -> p q s t u", q=QUADS, t=FRAMES),
+                )
+
+        def place_class(turned):
+            nc.scalar.copy(
+                out=side_grouped[0][:].bitcast(F32).rearrange("p (g r u) -> p g r u", g=PASSES, u=2),
+                in_=turned[:].rearrange("p (g u) r -> p g r u", u=2),
+            )
+
+        def place_loose(turned):
+            dst = side_grouped[1][:].bitcast(F32).rearrange("p (g l u) -> p g l u", g=PASSES, u=2)
+            src = turned[:].rearrange("p (g u) (q s) -> p g q s u", u=2, q=QUADS)
+            nc.scalar.copy(
+                out=dst[:, :, 0 : QUADS * LOOSE, :].rearrange("p g (q l) u -> p g q l u", q=QUADS),
+                in_=src[:, :, :, P // QUADS - LOOSE :, :],
+            )
+
+        def quantise_side(s):
+            nc.vector.quantize_mx(out=side_codes[s][:].bitcast(FP8X4), scales=side_scales[s][:], in_=side_grouped[s][:])
+
+        def quantise(k):
+            i, q = tiles[k]
+            first = q * SLOTS + i * P
+            for g in range(PASSES):
+                nc.vector.quantize_mx(
+                    out=codes[g][:, first : first + P].bitcast(FP8X4),
+                    scales=scales[g][:, first : first + P],
+                    in_=grouped[g][:, first * 4 : (first + P) * 4],
+                )
 
         def regroup_w(copy, g, first, last):
             copy(
@@ -176,16 +213,69 @@ def tile_timesformerlayer_pc_kernel(tc, ctx_s, x_res, s_out_w, s_out_b, out):
                     in_=w_grouped[g][:, halves[h], :].rearrange("p n t -> p (n t)"),
                 )
 
-        def multiply_patch(codes, scales, i):
+        def multiply_side(s):
+            banks = []
+            for h in range(HALVES):
+                acc = psum_acc.tile([P, BANK], F32, tag="acc")
+                for c in range(BANK // P):
+                    cols = slice(h * BANK + c * P, h * BANK + (c + 1) * P)
+                    for g in range(PASSES):
+                        rows = slice(g * P, (g + 1) * P)
+                        nc.tensor.matmul_mx(
+                            out=acc[:, c * P : (c + 1) * P],
+                            lhsT=w_codes[g][:, cols].bitcast(FP8X4),
+                            lhsT_scale=w_scales[g][:, cols],
+                            rhs=side_codes[s][:, rows].bitcast(FP8X4),
+                            rhs_scale=side_scales[s][:, rows],
+                            start=(g == 0),
+                            stop=(g == PASSES - 1),
+                        )
+                banks.append(acc)
+            return banks
+
+        def gather_side(s, banks):
+            per_bank = CHUNKS // HALVES
+            for h in range(HALVES):
+                dst = side_sums[s][:].rearrange("p (b c) -> p c b", c=CHUNKS)[:, h * per_bank : (h + 1) * per_bank, :]
+                if s == 0:
+                    nc.vector.tensor_reduce(
+                        out=dst,
+                        in_=banks[h][:].rearrange("p (c b t) -> p c b t", c=per_bank, t=FRAMES),
+                        axis=mybir.AxisListType.X,
+                        op=ADD,
+                    )
+                else:
+                    nc.vector.tensor_copy(
+                        out=dst, in_=banks[h][:].rearrange("p (c l) -> p c l", c=per_bank)[:, :, 0 : QUADS * LOOSE]
+                    )
+
+        def back_side(s):
+            back = psum_acc.tile([P, BANK], F32, tag="acc")
+            nc.tensor.transpose(out=back[:, 0:P], in_=side_sums[s][:], identity=ident[:])
+            return back
+
+        def finish_side(s, back):
+            nc.vector.scalar_tensor_tensor(
+                out=side_y[s][:],
+                in0=back[:, 0:P],
+                scalar=1.0 / FRAMES if s == 0 else 1.0,
+                in1=side_y[s][:],
+                op0=MULT,
+                op1=ADD,
+            )
+            nc.sync.dma_start(out=class_rows(out) if s == 0 else loose_rows(out), in_=side_y[s][:])
+
+        def multiply(k):
+            i, q = tiles[k]
+            first = q * SLOTS + i * P
             banks = []
             for h in range(HALVES):
                 acc = psum_acc.tile([P, BANK], F32, tag="acc")
                 for g in range(PASSES):
-                    rows = slice((i * PASSES + g) * P, (i * PASSES + g + 1) * P)
                     nc.tensor.matmul_mx(
                         out=acc[:],
-                        lhsT=codes[:, rows].bitcast(FP8X4),
-                        lhsT_scale=scales[:, rows],
+                        lhsT=codes[g][:, first : first + P].bitcast(FP8X4),
+                        lhsT_scale=scales[g][:, first : first + P],
                         rhs=w_codes[g][:, halves[h]].bitcast(FP8X4),
                         rhs_scale=w_scales[g][:, halves[h]],
                         start=(g == 0),
@@ -194,75 +284,81 @@ def tile_timesformerlayer_pc_kernel(tc, ctx_s, x_res, s_out_w, s_out_b, out):
                 banks.append(acc)
             return banks
 
-        def finish_patch(p, banks):
+        def finish(k, banks):
+            i, q = tiles[k]
+            for h in range(HALVES):
+                nc.vector.tensor_tensor(out=y[k][:, halves[h]], in0=banks[h][:], in1=y[k][:, halves[h]], op=ADD)
+            nc.sync.dma_start(out=window(out, i)[:, q, :], in_=y[k][:])
+
+        def class_back(k):
+            i, q = tiles[k]
+            r = class_at[i]
+            row = q * QUAD_ROWS + (i + 1) * ROWS
+            nc.sync.dma_start(out=y[k][r : r + 1, :], in_=rows_of(out)[row : row + 1, :])
+
+        def add_bias_vector(k, bias_psum):
+            i, q = tiles[k]
             for h in range(HALVES):
                 nc.vector.tensor_tensor(
-                    out=y_patch[p][:, halves[h]], in0=banks[h][:], in1=y_patch[p][:, halves[h]], op=ADD
+                    out=y[k][:, halves[h]], in0=bias_psum[h][:], in1=x_win[i][:, q, halves[h]], op=ADD
                 )
-                nc.sync.dma_start(out=patch_rows(out, p)[:, :, halves[h]], in_=y_patch[p][:, halves[h]])
 
-        def multiply_class(codes, scales, i):
-            banks = []
+        def add_bias_tensor(k):
+            i, q = tiles[k]
             for h in range(HALVES):
-                acc = psum_acc.tile([P, BANK], F32, tag="acc")
-                for q in range(BANK // P):
-                    cols = slice(h * BANK + q * P, h * BANK + (q + 1) * P)
-                    for g in range(PASSES):
-                        rows = slice((i * PASSES + g) * P, (i * PASSES + g + 1) * P)
-                        nc.tensor.matmul_mx(
-                            out=acc[:, q * P : (q + 1) * P],
-                            lhsT=w_codes[g][:, cols].bitcast(FP8X4),
-                            lhsT_scale=w_scales[g][:, cols],
-                            rhs=codes[:, rows].bitcast(FP8X4),
-                            rhs_scale=scales[:, rows],
-                            start=(g == 0),
-                            stop=(g == PASSES - 1),
-                        )
-                banks.append(acc)
-            return banks
-
-        def finish_class(banks):
-            per_bank = BANK // FRAMES
-            for h in range(HALVES):
-                nc.vector.tensor_reduce(
-                    out=class_sums[:, h * per_bank : (h + 1) * per_bank],
-                    in_=banks[h][:].rearrange("p (cb t) -> p cb t", t=FRAMES),
-                    axis=mybir.AxisListType.X,
-                    op=ADD,
+                both = psum_x.tile([P, BANK], F32, tag="x")
+                nc.tensor.matmul(
+                    out=both[:], lhsT=spread[i][:], rhs=x_win[i][:, q, halves[h]], start=True, stop=True
                 )
-            back = psum_turn.tile([P, BLOCKS, P], F32, tag="turned")
-            nc.tensor.transpose(out=back[:, 0, :], in_=class_sums[:], identity=ident[:])
-            nc.vector.scalar_tensor_tensor(
-                out=y_class[:], in0=back[:, 0, :], scalar=1.0 / FRAMES, in1=y_class[:], op0=MULT, op1=ADD
-            )
-            nc.sync.dma_start(out=class_rows(out), in_=y_class[:])
+                nc.scalar.copy(out=y[k][:, halves[h]], in_=both[:])
 
-        def multiply(tokens, codes, scales):
-            return [
-                multiply_class(codes, scales, i) if j == 0 else multiply_patch(codes, scales, i)
-                for i, j in enumerate(tokens)
-            ]
-
-        def finish(tokens, banks):
-            for i, j in enumerate(tokens):
-                if j == 0:
-                    finish_class(banks[i])
-                else:
-                    finish_patch(j - 1, banks[i])
-
-        n_groups = len(token_groups)
-        for g in range(PASSES):
-            prepare_w(g)
-        quantised = {}
-        for u in range(2):
-            quantised[u] = quantise(token_groups[u], turn(token_groups[u]))
-            add_bias(token_groups[u])
-        for u in range(n_groups):
-            codes, scales = quantised[u]
-            banks = multiply(token_groups[u], codes, scales)
-            if u + 2 < n_groups:
-                grouped = turn(token_groups[u + 2])
-                add_bias(token_groups[u + 2])
-            finish(token_groups[u], banks)
-            if u + 2 < n_groups:
-                quantised[u + 2] = quantise(token_groups[u + 2], grouped)
+        nc.vector.tensor_copy(out=bias_rows[0:1, :], in_=bias_row[:])
+        bias_psum = []
+        for h in range(HALVES):
+            both = psum_x.tile([P, BANK], F32, tag="x")
+            nc.tensor.matmul(out=both[:], lhsT=ones[:], rhs=bias_rows[:, halves[h]], start=True, stop=True)
+            bias_psum.append(both)
+        prepare_w(0)
+        for s in range(2):
+            nc.vector.tensor_tensor(out=side_y[s][:], in0=side_x[s][:], in1=bias_idx[:], op=ADD)
+        prepare_w(1)
+        place_class(turn(0))
+        quantise_side(0)
+        place(1, turn(1), nc.scalar.copy)
+        place(11, turn(11), nc.scalar.copy)
+        turned = turn(12)
+        place_loose(turned)
+        place(12, turned, nc.scalar.copy)
+        quantise_side(1)
+        class_banks = multiply_side(0)
+        for j in (2, 3, 4):
+            place(j, turn(j), nc.scalar.copy)
+        loose_banks = multiply_side(1)
+        gather_side(0, class_banks)
+        add_bias_vector(0, bias_psum)
+        gather_side(1, loose_banks)
+        for j in (5, 6):
+            place(j, turn(j), nc.scalar.copy)
+        finish_side(0, back_side(0))
+        add_bias_vector(1, bias_psum)
+        for j in (7, 8):
+            place(j, turn(j), nc.scalar.copy)
+        finish_side(1, back_side(1))
+        add_bias_vector(2, bias_psum)
+        add_bias_vector(3, bias_psum)
+        for k in range(on_vector):
+            class_back(k)
+        load_bias_row(1)
+        load_bias_row(2)
+        for j in (9, 10):
+            place(j, turn(j), nc.scalar.copy)
+        quantise(0)
+        for k in range(len(tiles)):
+            banks = multiply(k)
+            if on_vector <= k + lead < len(tiles):
+                add_bias_tensor(k + lead)
+            if k + 1 < len(tiles):
+                quantise(k + 1)
+            finish(k, banks)
+            if on_vector <= k + lead < len(tiles):
+                class_back(k + lead)

@@ -46,7 +46,7 @@ def tile_timesformerlayer_pc_kernel(tc, ctx_s, x_res, s_out_w, s_out_b, out):
     class_at = [ROWS * (i + 1) - 1 - P * i for i in range(WINDOWS)]
     tiles = [(i, q) for i in range(WINDOWS) for q in range(QUADS)]
     on_vector = 4
-    lead = 3
+    lead = 4
 
     with ExitStack() as stack:
         keep = stack.enter_context(tc.tile_pool(name="keep", bufs=1))
@@ -141,7 +141,7 @@ def tile_timesformerlayer_pc_kernel(tc, ctx_s, x_res, s_out_w, s_out_b, out):
 
         def load_bias_row(i):
             r = class_at[i]
-            nc.sync.dma_start(
+            nc.gpsimd.dma_start(
                 out=x_win[i][r : r + 1, :, :],
                 in_=s_out_b.rearrange("(o q n) -> o q n", o=1, q=1).to_broadcast([1, QUADS, D]),
             )
@@ -263,7 +263,7 @@ def tile_timesformerlayer_pc_kernel(tc, ctx_s, x_res, s_out_w, s_out_b, out):
                 op0=MULT,
                 op1=ADD,
             )
-            nc.sync.dma_start(out=class_rows(out) if s == 0 else loose_rows(out), in_=side_y[s][:])
+            nc.gpsimd.dma_start(out=class_rows(out) if s == 0 else loose_rows(out), in_=side_y[s][:])
 
         def multiply(k):
             i, q = tiles[k]
@@ -294,7 +294,7 @@ def tile_timesformerlayer_pc_kernel(tc, ctx_s, x_res, s_out_w, s_out_b, out):
             i, q = tiles[k]
             r = class_at[i]
             row = q * QUAD_ROWS + (i + 1) * ROWS
-            nc.sync.dma_start(out=y[k][r : r + 1, :], in_=rows_of(out)[row : row + 1, :])
+            nc.scalar.dma_start(out=y[k][r : r + 1, :], in_=rows_of(out)[row : row + 1, :])
 
         def add_bias_vector(k, bias_psum):
             i, q = tiles[k]
@@ -346,19 +346,18 @@ def tile_timesformerlayer_pc_kernel(tc, ctx_s, x_res, s_out_w, s_out_b, out):
         finish_side(1, back_side(1))
         add_bias_vector(2, bias_psum)
         add_bias_vector(3, bias_psum)
-        for k in range(on_vector):
-            class_back(k)
         load_bias_row(1)
         load_bias_row(2)
         for j in (9, 10):
             place(j, turn(j), nc.scalar.copy)
+        for k in range(on_vector):
+            class_back(k)
         quantise(0)
         for k in range(len(tiles)):
             banks = multiply(k)
             if on_vector <= k + lead < len(tiles):
                 add_bias_tensor(k + lead)
+                class_back(k + lead)
             if k + 1 < len(tiles):
                 quantise(k + 1)
             finish(k, banks)
-            if on_vector <= k + lead < len(tiles):
-                class_back(k + lead)

@@ -45,14 +45,13 @@ def tile_timesformerlayer_pc_kernel(tc, ctx_s, x_res, s_out_w, s_out_b, out):
     chunks = [(0, 2), (11, 2), (2, 3), (5, 3), (8, 2), (10, 1)]
     class_at = [ROWS * (i + 1) - 1 - P * i for i in range(WINDOWS)]
     tiles = [(i, q) for i in range(WINDOWS) for q in range(QUADS)]
-    on_vector = 4
+    adder = "VVGGGTTTTTTT"
     lead = 4
 
     with ExitStack() as stack:
         keep = stack.enter_context(tc.tile_pool(name="keep", bufs=1))
         psum_x = stack.enter_context(tc.psum_pool(name="psum_x", bufs=2))
-        psum_turn = stack.enter_context(tc.psum_pool(name="psum_turn", bufs=2))
-        psum_acc = stack.enter_context(tc.psum_pool(name="psum_acc", bufs=4))
+        psum_acc = stack.enter_context(tc.psum_pool(name="psum_acc", bufs=6))
         stack.enter_context(tc.manual_schedule())
 
         ident = keep.tile([P, P], F32)
@@ -62,6 +61,7 @@ def tile_timesformerlayer_pc_kernel(tc, ctx_s, x_res, s_out_w, s_out_b, out):
         bias_row = keep.tile([1, D], BF16)
         bias_rows = keep.tile([P, D], BF16)
         bias_idx = keep.tile([P, P], BF16)
+        bias_sbuf = keep.tile([P, D], F32)
         ctx_chunks = [keep.tile([P, n * D], BF16, name="ctx%d" % first) for first, n in chunks]
         w_raw = [keep.tile([P, 4, D], BF16, name="w_raw%d" % g) for g in range(PASSES)]
         w_grouped = [keep.tile([P, D, 4], BF16, name="w_grouped%d" % g, align_bytes=64) for g in range(PASSES)]
@@ -78,14 +78,18 @@ def tile_timesformerlayer_pc_kernel(tc, ctx_s, x_res, s_out_w, s_out_b, out):
         side_x = [keep.tile([P, P], BF16, name="side_x%d" % s) for s in range(2)]
         side_y = [keep.tile([P, P], F32, name="side_y%d" % s) for s in range(2)]
         side_sums = [keep.tile([P, P], F32, name="side_sums%d" % s) for s in range(2)]
-        x_win = [keep.tile([P, QUADS, D], BF16, name="x_win%d" % i) for i in range(WINDOWS)]
+        x_pair = [keep.tile([P, 2, D], BF16, name="x_pair%d" % n) for n in range(len(tiles) // 2)]
         y = [keep.tile([P, D], F32, name="y%d" % k) for k in range(len(tiles))]
 
         def rows_of(dram):
             return dram.rearrange("b j d -> (b j) d")
 
-        def class_rows(dram):
-            return dram[:, 0, :].rearrange("b (c n) -> b c n", n=P)
+        def class_rows(dram, s):
+            rows = rows_of(dram).rearrange("(q r) d -> q r d", q=QUADS)[:, s * ROWS, :]
+            return rows.rearrange("q (c n) -> q c n", n=P)
+
+        def class_part(tile, s):
+            return tile[s * QUADS * CHUNKS : (s + 1) * QUADS * CHUNKS, :]
 
         def loose_rows(dram):
             quads = rows_of(dram).rearrange("(q r) d -> q r d", q=QUADS)
@@ -107,7 +111,8 @@ def tile_timesformerlayer_pc_kernel(tc, ctx_s, x_res, s_out_w, s_out_b, out):
             )
 
         nc.sync.dma_start(out=bias_row[:], in_=s_out_b.rearrange("(o n) -> o n", o=1))
-        nc.scalar.dma_start(out=side_x[0][:], in_=class_rows(x_res))
+        for s in range(4):
+            nc.scalar.dma_start(out=class_part(side_x[0], s), in_=class_rows(x_res, s))
         nc.scalar.dma_start(
             out=bias_idx[:],
             in_=s_out_b.rearrange("(o c n) -> o c n", o=1, n=P).to_broadcast([SAMPLES, CHUNKS, P]),
@@ -126,8 +131,9 @@ def tile_timesformerlayer_pc_kernel(tc, ctx_s, x_res, s_out_w, s_out_b, out):
             first = 1 + P * i
             return rows_of(dram).rearrange("(q r) d -> r q d", q=QUADS)[first : first + P, :, :]
 
-        def load_x(i):
-            nc.sync.dma_start(out=x_win[i][:], in_=window(x_res, i))
+        def load_x(n):
+            i, q = tiles[2 * n]
+            nc.sync.dma_start(out=x_pair[n][:], in_=window(x_res, i)[:, q : q + 2, :])
 
         load_w(0)
         load_w(1)
@@ -136,14 +142,14 @@ def tile_timesformerlayer_pc_kernel(tc, ctx_s, x_res, s_out_w, s_out_b, out):
         load_x(0)
         for c in range(3, len(chunks)):
             load_ctx(c)
-        load_x(1)
-        load_x(2)
+        for n in range(1, len(tiles) // 2):
+            load_x(n)
 
-        def load_bias_row(i):
-            r = class_at[i]
-            nc.gpsimd.dma_start(
-                out=x_win[i][r : r + 1, :, :],
-                in_=s_out_b.rearrange("(o q n) -> o q n", o=1, q=1).to_broadcast([1, QUADS, D]),
+        def load_bias_rows(first, n):
+            r = class_at[tiles[first][0]]
+            nc.sync.dma_start(
+                out=x_pair[first // 2][r : r + 1, first % 2 : first % 2 + n, :],
+                in_=s_out_b.rearrange("(o q n) -> o q n", o=1, q=1).to_broadcast([1, n, D]),
             )
 
         def turn(j):
@@ -151,7 +157,7 @@ def tile_timesformerlayer_pc_kernel(tc, ctx_s, x_res, s_out_w, s_out_b, out):
                 if first <= j < first + n:
                     words = ctx_chunks[c][:].bitcast(F32)
                     base = (j - first) * WORDS
-            turned = psum_turn.tile([P, BLOCKS, P], F32, tag="turned")
+            turned = psum_acc.tile([P, BLOCKS, P], F32, tag="acc")
             for blk in range(BLOCKS):
                 at = base + (blk // 2) * 2 * P + blk % 2
                 nc.tensor.transpose(
@@ -236,15 +242,17 @@ def tile_timesformerlayer_pc_kernel(tc, ctx_s, x_res, s_out_w, s_out_b, out):
         def gather_side(s, banks):
             per_bank = CHUNKS // HALVES
             for h in range(HALVES):
-                dst = side_sums[s][:].rearrange("p (b c) -> p c b", c=CHUNKS)[:, h * per_bank : (h + 1) * per_bank, :]
+                pieces = slice(h * per_bank, (h + 1) * per_bank)
                 if s == 0:
+                    dst = side_sums[s][:].rearrange("p (s q c) -> p c q s", q=QUADS, c=CHUNKS)[:, pieces, :, :]
                     nc.vector.tensor_reduce(
                         out=dst,
-                        in_=banks[h][:].rearrange("p (c b t) -> p c b t", c=per_bank, t=FRAMES),
+                        in_=banks[h][:].rearrange("p (c q s t) -> p c q s t", c=per_bank, q=QUADS, t=FRAMES),
                         axis=mybir.AxisListType.X,
                         op=ADD,
                     )
                 else:
+                    dst = side_sums[s][:].rearrange("p (l c) -> p c l", c=CHUNKS)[:, pieces, :]
                     nc.vector.tensor_copy(
                         out=dst, in_=banks[h][:].rearrange("p (c l) -> p c l", c=per_bank)[:, :, 0 : QUADS * LOOSE]
                     )
@@ -263,7 +271,9 @@ def tile_timesformerlayer_pc_kernel(tc, ctx_s, x_res, s_out_w, s_out_b, out):
                 op0=MULT,
                 op1=ADD,
             )
-            nc.gpsimd.dma_start(out=class_rows(out) if s == 0 else loose_rows(out), in_=side_y[s][:])
+
+        def store_class(s):
+            nc.sync.dma_start(out=class_rows(out, s), in_=class_part(side_y[0], s))
 
         def multiply(k):
             i, q = tiles[k]
@@ -296,11 +306,19 @@ def tile_timesformerlayer_pc_kernel(tc, ctx_s, x_res, s_out_w, s_out_b, out):
             row = q * QUAD_ROWS + (i + 1) * ROWS
             nc.scalar.dma_start(out=y[k][r : r + 1, :], in_=rows_of(out)[row : row + 1, :])
 
+        def x_of(k):
+            return x_pair[k // 2][:, k % 2, :]
+
         def add_bias_vector(k, bias_psum):
-            i, q = tiles[k]
             for h in range(HALVES):
                 nc.vector.tensor_tensor(
-                    out=y[k][:, halves[h]], in0=bias_psum[h][:], in1=x_win[i][:, q, halves[h]], op=ADD
+                    out=y[k][:, halves[h]], in0=bias_psum[h][:], in1=x_of(k)[:, halves[h]], op=ADD
+                )
+
+        def add_bias_gpsimd(k):
+            for h in range(HALVES):
+                nc.gpsimd.tensor_tensor(
+                    out=y[k][:, halves[h]], in0=x_of(k)[:, halves[h]], in1=bias_sbuf[:, halves[h]], op=ADD
                 )
 
         def add_bias_tensor(k):
@@ -308,7 +326,7 @@ def tile_timesformerlayer_pc_kernel(tc, ctx_s, x_res, s_out_w, s_out_b, out):
             for h in range(HALVES):
                 both = psum_x.tile([P, BANK], F32, tag="x")
                 nc.tensor.matmul(
-                    out=both[:], lhsT=spread[i][:], rhs=x_win[i][:, q, halves[h]], start=True, stop=True
+                    out=both[:], lhsT=spread[i][:], rhs=x_of(k)[:, halves[h]], start=True, stop=True
                 )
                 nc.scalar.copy(out=y[k][:, halves[h]], in_=both[:])
 
@@ -318,6 +336,7 @@ def tile_timesformerlayer_pc_kernel(tc, ctx_s, x_res, s_out_w, s_out_b, out):
             both = psum_x.tile([P, BANK], F32, tag="x")
             nc.tensor.matmul(out=both[:], lhsT=ones[:], rhs=bias_rows[:, halves[h]], start=True, stop=True)
             bias_psum.append(both)
+            nc.scalar.copy(out=bias_sbuf[:, halves[h]], in_=both[:])
         prepare_w(0)
         for s in range(2):
             nc.vector.tensor_tensor(out=side_y[s][:], in0=side_x[s][:], in1=bias_idx[:], op=ADD)
@@ -330,34 +349,43 @@ def tile_timesformerlayer_pc_kernel(tc, ctx_s, x_res, s_out_w, s_out_b, out):
         place_loose(turned)
         place(12, turned, nc.scalar.copy)
         quantise_side(1)
-        class_banks = multiply_side(0)
         for j in (2, 3, 4):
-            place(j, turn(j), nc.scalar.copy)
-        loose_banks = multiply_side(1)
-        gather_side(0, class_banks)
+            place(j, turn(j), nc.vector.tensor_copy if j == 3 else nc.scalar.copy)
+        class_banks = multiply_side(0)
         add_bias_vector(0, bias_psum)
-        gather_side(1, loose_banks)
-        for j in (5, 6):
-            place(j, turn(j), nc.scalar.copy)
-        finish_side(0, back_side(0))
+        gather_side(0, class_banks)
+        for j in (5, 6, 7):
+            place(j, turn(j), nc.vector.tensor_copy if j == 6 else nc.scalar.copy)
         add_bias_vector(1, bias_psum)
-        for j in (7, 8):
-            place(j, turn(j), nc.scalar.copy)
-        finish_side(1, back_side(1))
-        add_bias_vector(2, bias_psum)
-        add_bias_vector(3, bias_psum)
-        load_bias_row(1)
-        load_bias_row(2)
-        for j in (9, 10):
-            place(j, turn(j), nc.scalar.copy)
-        for k in range(on_vector):
-            class_back(k)
+        for j in (8, 9, 10):
+            place(j, turn(j), nc.vector.tensor_copy if j == 9 else nc.scalar.copy)
+        finish_side(0, back_side(0))
+        store_class(0)
+        store_class(3)
+        loose_banks = multiply_side(1)
+        load_bias_rows(5, 1)
+        load_bias_rows(6, 2)
+        load_bias_rows(8, 2)
+        load_bias_rows(10, 2)
+        for k in (2, 3, 4):
+            add_bias_gpsimd(k)
         quantise(0)
+        quantise(1)
         for k in range(len(tiles)):
             banks = multiply(k)
-            if on_vector <= k + lead < len(tiles):
+            if k + lead < len(tiles) and adder[k + lead] == "T":
                 add_bias_tensor(k + lead)
-                class_back(k + lead)
-            if k + 1 < len(tiles):
-                quantise(k + 1)
+                if tiles[k + lead][0] == WINDOWS - 1:
+                    class_back(k + lead)
+            if k == 0:
+                gather_side(1, loose_banks)
+            if k == 1:
+                finish_side(1, back_side(1))
+                nc.sync.dma_start(out=loose_rows(out), in_=side_y[1][:])
+            if k + 2 < len(tiles):
+                quantise(k + 2)
             finish(k, banks)
+            if k == 6:
+                store_class(1)
+            if k == 10:
+                store_class(2)

@@ -26,6 +26,7 @@ HALVES = D // BANK
 CHUNKS = D // P
 WORDS = D // 2
 BLOCKS = WORDS // P
+PIECE = 256
 RUN = 4
 W_VECTOR_COLS = 384
 
@@ -45,8 +46,8 @@ def tile_timesformerlayer_pc_kernel(tc, ctx_s, x_res, s_out_w, s_out_b, out):
     chunks = [(0, 2), (11, 2), (2, 3), (5, 3), (8, 2), (10, 1)]
     class_at = [ROWS * (i + 1) - 1 - P * i for i in range(WINDOWS)]
     tiles = [(i, q) for i in range(WINDOWS) for q in range(QUADS)]
-    adder = "VVGGGTTTTTTT"
-    lead = 4
+    adder = "VGVGTTGTTTTT"
+    lead = 3
 
     with ExitStack() as stack:
         keep = stack.enter_context(tc.tile_pool(name="keep", bufs=1))
@@ -298,13 +299,16 @@ def tile_timesformerlayer_pc_kernel(tc, ctx_s, x_res, s_out_w, s_out_b, out):
             i, q = tiles[k]
             for h in range(HALVES):
                 nc.vector.tensor_tensor(out=y[k][:, halves[h]], in0=banks[h][:], in1=y[k][:, halves[h]], op=ADD)
-            nc.sync.dma_start(out=window(out, i)[:, q, :], in_=y[k][:])
+                if k == len(tiles) - 1:
+                    nc.sync.dma_start(out=window(out, i)[:, q, halves[h]], in_=y[k][:, halves[h]])
+            if k < len(tiles) - 1:
+                nc.sync.dma_start(out=window(out, i)[:, q, :], in_=y[k][:])
 
-        def class_back(k):
+        def class_back(engine, k):
             i, q = tiles[k]
             r = class_at[i]
             row = q * QUAD_ROWS + (i + 1) * ROWS
-            nc.scalar.dma_start(out=y[k][r : r + 1, :], in_=rows_of(out)[row : row + 1, :])
+            engine.dma_start(out=y[k][r : r + 1, :], in_=rows_of(out)[row : row + 1, :])
 
         def x_of(k):
             return x_pair[k // 2][:, k % 2, :]
@@ -316,10 +320,9 @@ def tile_timesformerlayer_pc_kernel(tc, ctx_s, x_res, s_out_w, s_out_b, out):
                 )
 
         def add_bias_gpsimd(k):
-            for h in range(HALVES):
-                nc.gpsimd.tensor_tensor(
-                    out=y[k][:, halves[h]], in0=x_of(k)[:, halves[h]], in1=bias_sbuf[:, halves[h]], op=ADD
-                )
+            for first in range(0, D, PIECE):
+                cols = slice(first, first + PIECE)
+                nc.gpsimd.tensor_tensor(out=y[k][:, cols], in0=x_of(k)[:, cols], in1=bias_sbuf[:, cols], op=ADD)
 
         def add_bias_tensor(k):
             i, q = tiles[k]
@@ -356,19 +359,17 @@ def tile_timesformerlayer_pc_kernel(tc, ctx_s, x_res, s_out_w, s_out_b, out):
         gather_side(0, class_banks)
         for j in (5, 6, 7):
             place(j, turn(j), nc.vector.tensor_copy if j == 6 else nc.scalar.copy)
-        add_bias_vector(1, bias_psum)
         for j in (8, 9, 10):
             place(j, turn(j), nc.vector.tensor_copy if j == 9 else nc.scalar.copy)
         finish_side(0, back_side(0))
+        loose_banks = multiply_side(1)
+        load_bias_rows(4, 2)
+        load_bias_rows(7, 1)
         store_class(0)
         store_class(3)
-        loose_banks = multiply_side(1)
-        load_bias_rows(5, 1)
-        load_bias_rows(6, 2)
-        load_bias_rows(8, 2)
-        load_bias_rows(10, 2)
-        for k in (2, 3, 4):
-            add_bias_gpsimd(k)
+        for k in range(len(tiles)):
+            if adder[k] == "G":
+                add_bias_gpsimd(k)
         quantise(0)
         quantise(1)
         for k in range(len(tiles)):
@@ -376,12 +377,18 @@ def tile_timesformerlayer_pc_kernel(tc, ctx_s, x_res, s_out_w, s_out_b, out):
             if k + lead < len(tiles) and adder[k + lead] == "T":
                 add_bias_tensor(k + lead)
                 if tiles[k + lead][0] == WINDOWS - 1:
-                    class_back(k + lead)
+                    class_back(nc.scalar, k + lead)
             if k == 0:
+                add_bias_vector(2, bias_psum)
                 gather_side(1, loose_banks)
             if k == 1:
-                finish_side(1, back_side(1))
+                loose_bank = back_side(1)
+            if k == 2:
+                load_bias_rows(8, 2)
+                finish_side(1, loose_bank)
                 nc.sync.dma_start(out=loose_rows(out), in_=side_y[1][:])
+            if k == 3:
+                load_bias_rows(10, 2)
             if k + 2 < len(tiles):
                 quantise(k + 2)
             finish(k, banks)

from contextlib import ExitStack

import concourse.mybir as mybir
from concourse.masks import make_identity

F32 = mybir.dt.float32
BF16 = mybir.dt.bfloat16
I32 = mybir.dt.int32
U32 = mybir.dt.uint32
U8 = mybir.dt.uint8
FP8X4 = mybir.dt.float8_e4m3fn_x4
ADD = mybir.AluOpType.add
MAX = mybir.AluOpType.max
MULT = mybir.AluOpType.mult

P = 128
SAMPLES = 16
FRAMES = 8
PATCHES = 12
TOKENS = 1 + PATCHES
D = 1024
K_PASS = 512
PASSES = D // K_PASS
BANK = 512
HALVES = D // BANK
CHUNKS = D // P
WORDS = D // 2
BLOCKS = WORDS // P
PIECE = 256
RUN = 4
W_VECTOR_COLS = 384

ROWS = 1 + PATCHES * FRAMES
QUADS = 4
QUAD_ROWS = 4 * ROWS
WINDOWS = 3
SLOTS = 512
LOOSE = 4

FLOPS = 2 * P * TOKENS * D * D


def tile_timesformerlayer_pc_kernel(tc, ctx_s, x_res, s_out_w, s_out_b, out):
    nc = tc.nc
    halves = [slice(h * BANK, (h + 1) * BANK) for h in range(HALVES)]
    chunks = [(0, 2), (11, 2), (2, 3), (5, 3), (8, 2), (10, 1)]
    class_at = [ROWS * (i + 1) - 1 - P * i for i in range(WINDOWS)]
    tiles = [(i, q) for i in range(WINDOWS) for q in range(QUADS)]
    adder = "VGVGTTGTTTTT"
    lead = 3

    with ExitStack() as stack:
        keep = stack.enter_context(tc.tile_pool(name="keep", bufs=1))
        psum_x = stack.enter_context(tc.psum_pool(name="psum_x", bufs=2))
        psum_acc = stack.enter_context(tc.psum_pool(name="psum_acc", bufs=6))
        stack.enter_context(tc.manual_schedule())

        ident = keep.tile([P, P], F32)
        ident_b = keep.tile([P, P], BF16)
        spread = [keep.tile([P, P], BF16, name="spread%d" % i) for i in range(WINDOWS)]
        ones = keep.tile([P, P], BF16)
        bias_row = keep.tile([1, D], BF16)
        bias_rows = keep.tile([P, D], BF16)
        bias_idx = keep.tile([P, P], BF16)
        bias_sbuf = keep.tile([P, D], F32)
        ctx_chunks = [keep.tile([P, n * D], BF16, name="ctx%d" % first) for first, n in chunks]
        w_raw = [keep.tile([P, 4, D], BF16, name="w_raw%d" % g) for g in range(PASSES)]
        w_grouped = [keep.tile([P, D, 4], BF16, name="w_grouped%d" % g, align_bytes=64) for g in range(PASSES)]
        w_codes = [keep.tile([P, D], U32, name="w_codes%d" % g, align_bytes=64) for g in range(PASSES)]
        w_scales = [keep.tile([P, D], U8, name="w_scales%d" % g, align_bytes=64) for g in range(PASSES)]
        grouped = [
            keep.tile([P, QUADS * SLOTS * 4], BF16, name="grouped%d" % g, align_bytes=64) for g in range(PASSES)
        ]
        codes = [keep.tile([P, QUADS * SLOTS], U32, name="codes%d" % g, align_bytes=64) for g in range(PASSES)]
        scales = [keep.tile([P, QUADS * SLOTS], U8, name="scales%d" % g, align_bytes=64) for g in range(PASSES)]
        side_grouped = [keep.tile([P, PASSES * P * 4], BF16, name="side_grouped%d" % s, align_bytes=64) for s in range(2)]
        side_codes = [keep.tile([P, PASSES * P], U32, name="side_codes%d" % s, align_bytes=64) for s in range(2)]
        side_scales = [keep.tile([P, PASSES * P], U8, name="side_scales%d" % s, align_bytes=64) for s in range(2)]
        side_x = [keep.tile([P, P], BF16, name="side_x%d" % s) for s in range(2)]
        side_y = [keep.tile([P, P], F32, name="side_y%d" % s) for s in range(2)]
        side_sums = [keep.tile([P, P], F32, name="side_sums%d" % s) for s in range(2)]
        x_pair = [keep.tile([P, 2, D], BF16, name="x_pair%d" % n) for n in range(len(tiles) // 2)]
        y = [keep.tile([P, D], F32, name="y%d" % k) for k in range(len(tiles))]

        def rows_of(dram):
            return dram.rearrange("b j d -> (b j) d")

        def class_rows(dram, s):
            rows = rows_of(dram).rearrange("(q r) d -> q r d", q=QUADS)[:, s * ROWS, :]
            return rows.rearrange("q (c n) -> q c n", n=P)

        def class_part(tile, s):
            return tile[s * QUADS * CHUNKS : (s + 1) * QUADS * CHUNKS, :]

        def loose_rows(dram):
            quads = rows_of(dram).rearrange("(q r) d -> q r d", q=QUADS)
            return quads[:, QUAD_ROWS - LOOSE :, :].rearrange("q r (c n) -> q (r c) n", n=P)

        nc.vector.memset(bias_rows[:].bitcast(I32), 0)
        nc.vector.memset(ones[:], 1.0)
        make_identity(nc, ident[:])
        nc.gpsimd.memset(side_grouped[1][:].bitcast(I32), 0)
        for g in range(PASSES):
            slots = grouped[g][:].rearrange("p (q l t) -> p q l t", q=QUADS, t=4)
            slots = slots[:, :, ROWS - 1 : WINDOWS * ROWS + ROWS - 1, :]
            nc.gpsimd.memset(slots.rearrange("p q (s l) t -> p q s l t", s=WINDOWS)[:, :, :, 0:1, :], 0.0)
        nc.gpsimd.tensor_copy(out=ident_b[:], in_=ident[:])
        for i in range(WINDOWS):
            r = class_at[i]
            nc.gpsimd.tensor_scalar(
                out=spread[i][:], in0=ident_b[:], scalar1=ident[:, r : r + 1], scalar2=None, op0=MAX
            )

        nc.sync.dma_start(out=bias_row[:], in_=s_out_b.rearrange("(o n) -> o n", o=1))
        for s in range(4):
            nc.scalar.dma_start(out=class_part(side_x[0], s), in_=class_rows(x_res, s))
        nc.scalar.dma_start(
            out=bias_idx[:],
            in_=s_out_b.rearrange("(o c n) -> o c n", o=1, n=P).to_broadcast([SAMPLES, CHUNKS, P]),
        )
        nc.scalar.dma_start(out=side_x[1][:], in_=loose_rows(x_res))

        def load_w(g):
            rows = s_out_w[g * K_PASS : (g + 1) * K_PASS, :]
            nc.sync.dma_start(out=w_raw[g][:], in_=rows.rearrange("(p t) n -> p t n", t=4))

        def load_ctx(c):
            first, n = chunks[c]
            nc.sync.dma_start(out=ctx_chunks[c][:], in_=ctx_s[:, first : first + n, :].rearrange("s j d -> s (j d)"))

        def window(dram, i):
            first = 1 + P * i
            return rows_of(dram).rearrange("(q r) d -> r q d", q=QUADS)[first : first + P, :, :]

        def load_x(n):
            i, q = tiles[2 * n]
            nc.sync.dma_start(out=x_pair[n][:], in_=window(x_res, i)[:, q : q + 2, :])

        load_w(0)
        load_w(1)
        for c in range(3):
            load_ctx(c)
        load_x(0)
        for c in range(3, len(chunks)):
            load_ctx(c)
        for n in range(1, len(tiles) // 2):
            load_x(n)

        def load_bias_rows(first, n):
            r = class_at[tiles[first][0]]
            nc.sync.dma_start(
                out=x_pair[first // 2][r : r + 1, first % 2 : first % 2 + n, :],
                in_=s_out_b.rearrange("(o q n) -> o q n", o=1, q=1).to_broadcast([1, n, D]),
            )

        def turn(j):
            for c, (first, n) in enumerate(chunks):
                if first <= j < first + n:
                    words = ctx_chunks[c][:].bitcast(F32)
                    base = (j - first) * WORDS
            turned = psum_acc.tile([P, BLOCKS, P], F32, tag="acc")
            for blk in range(BLOCKS):
                at = base + (blk // 2) * 2 * P + blk % 2
                nc.tensor.transpose(
                    out=turned[:, blk, :], in_=words[:, at : at + 2 * P - 1 : 2], identity=ident[:]
                )
            return turned

        def place(j, turned, copy):
            first = (j - 1) * FRAMES
            for g in range(PASSES):
                slots = grouped[g][:].bitcast(F32).rearrange("p (q l u) -> p q l u", q=QUADS, u=2)
                slots = slots[:, :, first : first + QUAD_ROWS, :].rearrange("p q (s l) u -> p q s l u", s=4)
                copy(
                    out=slots[:, :, :, 0:FRAMES, :],
                    in_=turned[:, 2 * g : 2 * g + 2, :].rearrange("p u (q s t) -> p q s t u", q=QUADS, t=FRAMES),
                )

        def place_class(turned):
            nc.scalar.copy(
                out=side_grouped[0][:].bitcast(F32).rearrange("p (g r u) -> p g r u", g=PASSES, u=2),
                in_=turned[:].rearrange("p (g u) r -> p g r u", u=2),
            )

        def place_loose(turned):
            dst = side_grouped[1][:].bitcast(F32).rearrange("p (g l u) -> p g l u", g=PASSES, u=2)
            src = turned[:].rearrange("p (g u) (q s) -> p g q s u", u=2, q=QUADS)
            nc.scalar.copy(
                out=dst[:, :, 0 : QUADS * LOOSE, :].rearrange("p g (q l) u -> p g q l u", q=QUADS),
                in_=src[:, :, :, P // QUADS - LOOSE :, :],
            )

        def quantise_side(s):
            nc.vector.quantize_mx(out=side_codes[s][:].bitcast(FP8X4), scales=side_scales[s][:], in_=side_grouped[s][:])

        def quantise(k):
            i, q = tiles[k]
            first = q * SLOTS + i * P
            for g in range(PASSES):
                nc.vector.quantize_mx(
                    out=codes[g][:, first : first + P].bitcast(FP8X4),
                    scales=scales[g][:, first : first + P],
                    in_=grouped[g][:, first * 4 : (first + P) * 4],
                )

        def regroup_w(copy, g, first, last):
            copy(
                out=w_grouped[g][:, first:last, :].rearrange("p (c i) t -> p c t i", i=RUN),
                in_=w_raw[g][:, :, first:last].rearrange("p t (c i) -> p c t i", i=RUN),
            )

        def prepare_w(g):
            for h in range(HALVES):
                regroup_w(nc.vector.tensor_copy, g, h * BANK, h * BANK + W_VECTOR_COLS)
                regroup_w(nc.scalar.copy, g, h * BANK + W_VECTOR_COLS, (h + 1) * BANK)
            for h in range(HALVES):
                nc.vector.quantize_mx(
                    out=w_codes[g][:, halves[h]].bitcast(FP8X4),
                    scales=w_scales[g][:, halves[h]],
                    in_=w_grouped[g][:, halves[h], :].rearrange("p n t -> p (n t)"),
                )

        def multiply_side(s):
            banks = []
            for h in range(HALVES):
                acc = psum_acc.tile([P, BANK], F32, tag="acc")
                for c in range(BANK // P):
                    cols = slice(h * BANK + c * P, h * BANK + (c + 1) * P)
                    for g in range(PASSES):
                        rows = slice(g * P, (g + 1) * P)
                        nc.tensor.matmul_mx(
                            out=acc[:, c * P : (c + 1) * P],
                            lhsT=w_codes[g][:, cols].bitcast(FP8X4),
                            lhsT_scale=w_scales[g][:, cols],
                            rhs=side_codes[s][:, rows].bitcast(FP8X4),
                            rhs_scale=side_scales[s][:, rows],
                            start=(g == 0),
                            stop=(g == PASSES - 1),
                        )
                banks.append(acc)
            return banks

        def gather_side(s, banks):
            per_bank = CHUNKS // HALVES
            for h in range(HALVES):
                pieces = slice(h * per_bank, (h + 1) * per_bank)
                if s == 0:
                    dst = side_sums[s][:].rearrange("p (s q c) -> p c q s", q=QUADS, c=CHUNKS)[:, pieces, :, :]
                    nc.vector.tensor_reduce(
                        out=dst,
                        in_=banks[h][:].rearrange("p (c q s t) -> p c q s t", c=per_bank, q=QUADS, t=FRAMES),
                        axis=mybir.AxisListType.X,
                        op=ADD,
                    )
                else:
                    dst = side_sums[s][:].rearrange("p (l c) -> p c l", c=CHUNKS)[:, pieces, :]
                    nc.vector.tensor_copy(
                        out=dst, in_=banks[h][:].rearrange("p (c l) -> p c l", c=per_bank)[:, :, 0 : QUADS * LOOSE]
                    )

        def back_side(s):
            back = psum_acc.tile([P, BANK], F32, tag="acc")
            nc.tensor.transpose(out=back[:, 0:P], in_=side_sums[s][:], identity=ident[:])
            return back

        def finish_side(s, back):
            nc.vector.scalar_tensor_tensor(
                out=side_y[s][:],
                in0=back[:, 0:P],
                scalar=1.0 / FRAMES if s == 0 else 1.0,
                in1=side_y[s][:],
                op0=MULT,
                op1=ADD,
            )

        def store_class(s):
            nc.sync.dma_start(out=class_rows(out, s), in_=class_part(side_y[0], s))

        def multiply(k):
            i, q = tiles[k]
            first = q * SLOTS + i * P
            banks = []
            for h in range(HALVES):
                acc = psum_acc.tile([P, BANK], F32, tag="acc")
                for g in range(PASSES):
                    nc.tensor.matmul_mx(
                        out=acc[:],
                        lhsT=codes[g][:, first : first + P].bitcast(FP8X4),
                        lhsT_scale=scales[g][:, first : first + P],
                        rhs=w_codes[g][:, halves[h]].bitcast(FP8X4),
                        rhs_scale=w_scales[g][:, halves[h]],
                        start=(g == 0),
                        stop=(g == PASSES - 1),
                    )
                banks.append(acc)
            return banks

        def finish(k, banks):
            i, q = tiles[k]
            for h in range(HALVES):
                nc.vector.tensor_tensor(out=y[k][:, halves[h]], in0=banks[h][:], in1=y[k][:, halves[h]], op=ADD)
                if k == len(tiles) - 1:
                    nc.sync.dma_start(out=window(out, i)[:, q, halves[h]], in_=y[k][:, halves[h]])
            if k < len(tiles) - 1:
                nc.sync.dma_start(out=window(out, i)[:, q, :], in_=y[k][:])

        def class_back(engine, k):
            i, q = tiles[k]
            r = class_at[i]
            row = q * QUAD_ROWS + (i + 1) * ROWS
            engine.dma_start(out=y[k][r : r + 1, :], in_=rows_of(out)[row : row + 1, :])

        def x_of(k):
            return x_pair[k // 2][:, k % 2, :]

        def add_bias_vector(k, bias_psum):
            for h in range(HALVES):
                nc.vector.tensor_tensor(
                    out=y[k][:, halves[h]], in0=bias_psum[h][:], in1=x_of(k)[:, halves[h]], op=ADD
                )

        def add_bias_gpsimd(k):
            for first in range(0, D, PIECE):
                cols = slice(first, first + PIECE)
                nc.gpsimd.tensor_tensor(out=y[k][:, cols], in0=x_of(k)[:, cols], in1=bias_sbuf[:, cols], op=ADD)

        def add_bias_tensor(k):
            i, q = tiles[k]
            for h in range(HALVES):
                both = psum_x.tile([P, BANK], F32, tag="x")
                nc.tensor.matmul(
                    out=both[:], lhsT=spread[i][:], rhs=x_of(k)[:, halves[h]], start=True, stop=True
                )
                nc.scalar.copy(out=y[k][:, halves[h]], in_=both[:])

        nc.vector.tensor_copy(out=bias_rows[0:1, :], in_=bias_row[:])
        bias_psum = []
        for h in range(HALVES):
            both = psum_x.tile([P, BANK], F32, tag="x")
            nc.tensor.matmul(out=both[:], lhsT=ones[:], rhs=bias_rows[:, halves[h]], start=True, stop=True)
            bias_psum.append(both)
            nc.scalar.copy(out=bias_sbuf[:, halves[h]], in_=both[:])
        prepare_w(0)
        for s in range(2):
            nc.vector.tensor_tensor(out=side_y[s][:], in0=side_x[s][:], in1=bias_idx[:], op=ADD)
        prepare_w(1)
        place_class(turn(0))
        quantise_side(0)
        place(1, turn(1), nc.scalar.copy)
        place(11, turn(11), nc.scalar.copy)
        turned = turn(12)
        place_loose(turned)
        place(12, turned, nc.scalar.copy)
        quantise_side(1)
        for j in (2, 3, 4):
            place(j, turn(j), nc.vector.tensor_copy if j == 3 else nc.scalar.copy)
        class_banks = multiply_side(0)
        add_bias_vector(0, bias_psum)
        gather_side(0, class_banks)
        for j in (5, 6, 7):
            place(j, turn(j), nc.vector.tensor_copy if j == 6 else nc.scalar.copy)
        for j in (8, 9, 10):
            place(j, turn(j), nc.vector.tensor_copy if j == 9 else nc.scalar.copy)
        finish_side(0, back_side(0))
        loose_banks = multiply_side(1)
        load_bias_rows(4, 2)
        load_bias_rows(7, 1)
        store_class(0)
        store_class(3)
        for k in range(len(tiles)):
            if adder[k] == "G":
                add_bias_gpsimd(k)
        quantise(0)
        quantise(1)
        for k in range(len(tiles)):
            banks = multiply(k)
            if k + lead < len(tiles) and adder[k + lead] == "T":
                add_bias_tensor(k + lead)
                if tiles[k + lead][0] == WINDOWS - 1:
                    class_back(nc.scalar, k + lead)
            if k == 0:
                add_bias_vector(2, bias_psum)
                gather_side(1, loose_banks)
            if k == 1:
                loose_bank = back_side(1)
            if k == 2:
                load_bias_rows(8, 2)
                finish_side(1, loose_bank)
                nc.sync.dma_start(out=loose_rows(out), in_=side_y[1][:])
            if k == 3:
                load_bias_rows(10, 2)
            if k + 2 < len(tiles):
                quantise(k + 2)
            finish(k, banks)
            if k == 6:
                store_class(1)
            if k == 10:
                store_class(2)
